import numpy as np
import ml_dtypes


def mxq(x, axis, fmt="e4m3"):
    dtype, down = {"e4m3": (ml_dtypes.float8_e4m3fn, 7), "e5m2": (ml_dtypes.float8_e5m2, 14)}[fmt]
    v = np.moveaxis(np.asarray(x, np.float32).astype(ml_dtypes.bfloat16).astype(np.float64), axis, -1)
    blocks = v.reshape(v.shape[:-1] + (-1, 32))
    amax = np.abs(blocks).max(-1, keepdims=True)
    byte = np.maximum(np.where(amax > 0, np.frexp(amax)[1] - 1 + 127, 0) - down, 1)
    scale = np.exp2(byte - 127.0)
    codes = (blocks / scale).astype(np.float32).astype(dtype).astype(np.float64)
    return np.moveaxis((codes * scale).reshape(v.shape), -1, axis)


WIDE = False


def mx_kscale(k):
    if not WIDE:
        return np.ones(k)
    levels = np.array([10, -10, 5, -5, 0])
    if k % 512:
        return np.exp2(np.random.permutation(np.resize(levels, k // 32))).repeat(32)
    a = np.empty((k // 512, 16))
    for p in range(k // 512):
        a[p, :8] = np.random.permutation(np.resize(levels, 8))
        for g in range(8):
            far = levels[np.abs(levels - a[p, g]) >= 10]
            a[p, g + 8] = far[np.random.randint(len(far))]
    return np.exp2(a.ravel()).repeat(32)


BF16 = ml_dtypes.bfloat16


def bf(x):
    return np.asarray(x, np.float32).astype(BF16)


def f64(x):
    return np.asarray(x).astype(np.float64)


B, S, D_MODEL, N_H, D_H, D_CQ, D_CKV, D_HR = 4, 1024, 1024, 4, 128, 512, 512, 128
ROPE_BASE = 10000.0


def rope_cos_sin(seq_len, dim):
    inv_freq = 1.0 / (ROPE_BASE ** (np.arange(0, dim, 2) / dim))
    ang = np.arange(seq_len)[:, None] * inv_freq[None, :]
    return np.cos(ang), np.sin(ang)


def rope(t, cos, sin):
    shp = t.shape
    d2 = shp[-1] // 2
    tr = t.reshape(shp[:-1] + (d2, 2))
    x0, x1 = tr[..., 0], tr[..., 1]
    bshape = (1, shp[1]) + (1,) * (x0.ndim - 3) + (d2,)
    cs, sn = cos.reshape(bshape), sin.reshape(bshape)
    return np.stack([x0 * cs - x1 * sn, x0 * sn + x1 * cs], axis=-1).reshape(shp)


def draw0():
    s, t = mx_kscale(D_MODEL), mx_kscale(D_CQ)
    return {"h": bf(np.random.standard_normal((B, S, D_MODEL)) * s),
            "w_cq": bf(np.random.standard_normal((D_MODEL, D_CQ)) / np.sqrt(D_MODEL) / s[:, None] * t),
            "w_q": bf(np.random.standard_normal((D_CQ, N_H * D_H)) / np.sqrt(D_CQ) / t[:, None]),
            "w_qr": bf(np.random.standard_normal((D_CQ, N_H * D_HR)) / np.sqrt(D_CQ) / t[:, None])}


def core(h, w_cq, w_q, w_qr):
    cos, sin = rope_cos_sin(S, D_HR)
    c_q = mxq(f64(h), 2, "e4m3") @ mxq(f64(w_cq), 0, "e4m3")
    cq = mxq(c_q, 2, "e4m3")
    q_c = (cq @ mxq(f64(w_q), 0, "e4m3")).reshape(B, S, N_H, D_H).transpose(0, 2, 1, 3)
    q_r = rope((cq @ mxq(f64(w_qr), 0, "e4m3")).reshape(B, S, N_H, D_HR), cos, sin).transpose(0, 2, 1, 3)
    return np.concatenate([q_c, q_r], axis=-1)


def e4m3fn_bytes(y):
    return np.clip(np.asarray(y, np.float64), -448.0, 448.0).astype(np.float32).astype(ml_dtypes.float8_e4m3fn).view(np.uint8)


def e4m3fn_values(b):
    return np.asarray(b, np.uint8).view(ml_dtypes.float8_e4m3fn).astype(np.float64)


def setup_inputs():
    d = draw0()
    x0 = np.asarray(d['h']).astype(np.float64)
    s = (np.max(np.abs(x0), axis=(0, 1), keepdims=True) / 448.0).astype(np.float32)
    out = {}
    for k, v in d.items():
        if k == 'h':
            out['h_bytes'] = e4m3fn_bytes(x0 / s.astype(np.float64))
            out['h_scale'] = s
        else:
            out[k] = v
    return out


def reference(h_bytes, h_scale, w_cq, w_q, w_qr):
    return core(e4m3fn_values(h_bytes) * h_scale.astype(np.float64), w_cq, w_q, w_qr)

@@ -1,0 +1,316 @@
+from contextlib import ExitStack
+import math
+
+import concourse.mybir as mybir
+from concourse.masks import make_identity
+
+F32 = mybir.dt.float32
+BF16 = mybir.dt.bfloat16
+U32 = mybir.dt.uint32
+I32 = mybir.dt.int32
+U8 = mybir.dt.uint8
+E4M3 = mybir.dt.float8_e4m3fn
+FP8X4 = mybir.dt.float8_e4m3fn_x4
+ALU = mybir.AluOpType
+ACT = mybir.ActivationFunctionType
+
+B, S, D, H, DH, CQ = 4, 1024, 1024, 4, 128, 512
+P = 128
+NT = B * S // P
+NC = NT // 4
+NP = NT // 2
+AHEAD = 3
+
+FLOPS = 2 * B * S * (D * CQ + 2 * CQ * H * DH) + 3 * B * S * H * DH
+
+
+def tile_mla_pa_t_kernel(tc, h_bytes, h_scale, w_cq, w_q, w_qr, out):
+    nc = tc.nc
+    with ExitStack() as ctx:
+        keep = ctx.enter_context(tc.tile_pool(name="keep", bufs=1))
+        work = ctx.enter_context(tc.tile_pool(name="work", bufs=3))
+        psum = ctx.enter_context(tc.psum_pool(name="psum", bufs=1))
+        ctx.enter_context(tc.manual_schedule())
+
+        hb = []
+        for c in range(NC):
+            t = keep.tile([P, 4, D], U8, name=f"hb{c}", align_bytes=64)
+            hb.append(t)
+
+        def load_h(c, j0, j1):
+            b, half = c // 2, c % 2
+            nc.sync.dma_start(
+                out=hb[c][:, j0:j1, :],
+                in_=h_bytes[b, half * 512 : (half + 1) * 512, :].rearrange("(p j) k -> p j k", j=4)[:, j0:j1, :],
+            )
+
+        sv = keep.tile([P, 8], F32, name="sv")
+        nc.sync.dma_start(out=sv[:], in_=h_scale.rearrange("a b (p c) -> p (a b c)", c=8))
+        wcq_raw = [keep.tile([P, 4, CQ], BF16, name=f"wcq_raw{g}", align_bytes=64) for g in range(2)]
+
+        def load_wcq(g):
+            nc.sync.dma_start(out=wcq_raw[g][:],
+                              in_=w_cq[g * 512 : (g + 1) * 512, :].rearrange("(p j) c -> p j c", j=4))
+
+        wq_raw = keep.tile([P, 4, H * DH], BF16, name="wq_raw", align_bytes=64)
+        wqr_raw = keep.tile([P, 4, H * DH], BF16, name="wqr_raw", align_bytes=64)
+        load_wcq(0)
+        load_h(0, 0, 2)
+        load_wcq(1)
+        load_h(0, 2, 4)
+        nc.sync.dma_start(out=wq_raw[:], in_=w_q.rearrange("(p j) c -> p j c", j=4))
+        load_h(1, 0, 4)
+        nc.sync.dma_start(out=wqr_raw[:], in_=w_qr.rearrange("(p j) c -> p j c", j=4))
+        for c in range(2, NC):
+            load_h(c, 0, 4)
+
+        ident = keep.tile([P, P], F32, name="ident", align_bytes=64)
+        make_identity(nc, ident[:])
+        warm = keep.tile([P, 1], F32, name="warm")
+        nc.gpsimd.memset(warm[:], 0.0)
+        warm2 = keep.tile([P, 1], F32, name="warm2")
+        nc.scalar.activation(out=warm2[:], in_=warm[:], func=ACT.Sin)
+        th = keep.tile([P, 64], F32, name="th")
+        nc.gpsimd.memset(th[:, 0:1], 1.0)
+        w = 1
+        while w < 64:
+            nc.gpsimd.tensor_scalar(out=th[:, w : 2 * w], in0=th[:, 0:w], scalar1=10000.0 ** (-w / 64.0),
+                                    scalar2=None, op0=ALU.mult)
+            w *= 2
+        th2 = keep.tile([P, P], F32, name="th2", align_bytes=64)
+        for e in range(2):
+            nc.gpsimd.tensor_scalar(out=th2[:].rearrange("p (i two) -> p two i", two=2)[:, e, :], in0=th[:],
+                                    scalar1=(1.0 - 2.0 * e) / (2.0 * math.pi), scalar2=None, op0=ALU.mult)
+        s_row = keep.tile([P, S], F32, name="s_row", align_bytes=64)
+        nc.gpsimd.iota(s_row[:].rearrange("p (c j q) -> p c j q", c=2, j=4), pattern=[[512, 2], [1, 4], [4, 128]],
+                       base=0, channel_multiplier=0, allow_small_or_imprecise_dtypes=True)
+        hpi = keep.tile([P, 1], F32, name="hpi")
+        nc.gpsimd.memset(hpi[:], 1.0)
+        hpi2 = keep.tile([P, 1], F32, name="hpi2")
+        nc.gpsimd.tensor_scalar(out=hpi2[:], in0=hpi[:], scalar1=math.pi / 2, scalar2=None, op0=ALU.mult)
+        perm = keep.tile([P, P], F32, name="perm", align_bytes=64)
+        for e in range(2):
+            nc.gpsimd.tensor_copy(out=perm[:].rearrange("p (i two) -> p two i", two=2)[:, e, :],
+                                  in_=ident[:].rearrange("p (i two) -> p two i", two=2)[:, 1 - e, :])
+
+        scale = keep.tile([P, 2, D], F32, name="scale", align_bytes=64)
+        sc_ps = [psum.tile([P, 4, P], F32, name=f"sc_ps{k}", tag="ht", bufs=2) for k in range(2)]
+        for k in range(8):
+            nc.tensor.transpose(sc_ps[k // 4][:, k % 4, :], sv[:, k : k + 1].to_broadcast([P, P]), ident[:])
+        scv = scale[:].rearrange("p r (q k c) -> p r k q c", k=2, c=4)
+        for r in range(2):
+            nc.vector.tensor_copy(out=scv[:, r, 0], in_=sc_ps[0][:].rearrange("p c q -> p q c"))
+            nc.scalar.copy(out=scv[:, r, 1], in_=sc_ps[1][:].rearrange("p c q -> p q c"))
+
+        th_ps = psum.tile([P, P], F32, name="th_ps", tag="ra", bufs=2)
+        thc = keep.tile([P, 1], F32, name="thc")
+        turns = keep.tile([P, S], F32, name="turns", align_bytes=64)
+        whole = keep.tile([P, S], I32, name="whole", align_bytes=64)
+        frac = keep.tile([P, S], F32, name="frac", align_bytes=64)
+        fabs = keep.tile([P, S], F32, name="fabs", align_bytes=64)
+        tab = keep.tile([P, 2, 2, 512], F32, name="tab", align_bytes=64)
+
+        def turns_g():
+            nc.tensor.transpose(th_ps[:], th2[:], ident[:])
+            nc.scalar.copy(out=thc[:], in_=th_ps[:, 0:1])
+            nc.gpsimd.tensor_scalar(out=turns[:], in0=s_row[:], scalar1=thc[:, 0:1], scalar2=0.0,
+                                    op0=ALU.mult, op1=ALU.add)
+
+        def tables_v():
+            nc.vector.tensor_copy(out=whole[:], in_=turns[:])
+            nc.vector.tensor_tensor(out=frac[:], in0=turns[:], in1=whole[:], op=ALU.subtract)
+
+        def tables_s():
+            fr = frac[:].rearrange("p (h q) -> p h q", h=2)
+            fa = fabs[:].rearrange("p (h q) -> p h q", h=2)
+            nc.scalar.activation(out=tab[:, :, 1, :], in_=fr, func=ACT.Sin, scale=2.0 * math.pi)
+            nc.scalar.activation(out=fa, in_=fr, func=ACT.Abs)
+            nc.scalar.activation(out=tab[:, :, 0, :], in_=fa, func=ACT.Sin, scale=-2.0 * math.pi, bias=hpi2[:, 0:1])
+
+        wcq_codes = keep.tile([P, 2, CQ], U32, name="wcq_codes", align_bytes=64)
+        wcq_sc = keep.tile([P, 2, CQ], U8, name="wcq_sc", align_bytes=64)
+        wq_codes = keep.tile([P, 512], U32, name="wq_codes", align_bytes=64)
+        wq_sc = keep.tile([P, 512], U8, name="wq_sc", align_bytes=64)
+        wqr_codes = keep.tile([P, 512], U32, name="wqr_codes", align_bytes=64)
+        wqr_sc = keep.tile([P, 512], U8, name="wqr_sc", align_bytes=64)
+        wcq_g = [keep.tile([P, 4 * CQ], BF16, name=f"wcq_g{g}", align_bytes=64) for g in range(2)]
+        wq_g = keep.tile([P, 2048], BF16, name="wq_g", align_bytes=64)
+        wqr_g = keep.tile([P, 2048], BF16, name="wqr_g", align_bytes=64)
+
+        def wcq_copy(copy, g):
+            copy(out=wcq_g[g][:].rearrange("p (t m j) -> p t m j", t=4, j=4),
+                 in_=wcq_raw[g][:].rearrange("p j (m t) -> p t m j", t=4))
+
+        def wcq_quant(g):
+            nc.vector.quantize_mx(out=wcq_codes[:, g, :].bitcast(FP8X4), scales=wcq_sc[:, g, :], in_=wcq_g[g][:])
+
+        def w_copy(copy, grouped, raw):
+            copy(out=grouped[:].rearrange("p (n j) -> p n j", j=4), in_=raw[:].rearrange("p j n -> p n j"))
+
+        xb, hps, grp, hq, cps, cgs, ccodes, ups, ts, rps, aps, osb = ({} for k in range(12))
+
+        def widen(q):
+            if not 0 <= q < NP:
+                return
+            j = 2 * (q % 2)
+            x = work.tile([P, 2, D], BF16, name=f"x{q}", tag="x", bufs=AHEAD + 2, align_bytes=64)
+            nc.vector.tensor_tensor(out=x[:], in0=hb[q // 2][:, j : j + 2, :].bitcast(E4M3), in1=scale[:], op=ALU.mult)
+            xb[q] = x
+
+        def h_transpose(q):
+            for i in range(2):
+                ht = psum.tile([P, 2, 2, P], F32, name=f"ht{q}_{i}", tag="ht", bufs=2)
+                words = xb[q][:, i, :].bitcast(F32)
+                for g in range(2):
+                    for u in range(2):
+                        nc.tensor.transpose(ht[:, g, u, :], words[:, 256 * g + u : 256 * (g + 1) : 2], ident[:])
+                hps[q, i] = ht
+
+        def h_copy(q):
+            gt = work.tile([P, 2, D], BF16, name=f"g{q}", tag="g", align_bytes=64)
+            for i in range(2):
+                nc.scalar.copy(out=gt[:, i, :].bitcast(F32).rearrange("p (g n u) -> p g n u", g=2, u=2),
+                               in_=hps[q, i][:].rearrange("p g u n -> p g n u"))
+            grp[q] = gt
+
+        def h_quant(q):
+            codes = work.tile([P, 512], U32, name=f"hc{q}", tag="hc", align_bytes=64)
+            sc = work.tile([P, 512], U8, name=f"hs{q}", tag="hs", align_bytes=64)
+            nc.vector.quantize_mx(out=codes[:].bitcast(FP8X4), scales=sc[:],
+                                  in_=grp[q][:].rearrange("p i k -> p (i k)"))
+            hq[q] = (codes, sc)
+
+        def mm1(q):
+            codes, sc = hq[q]
+            for i in range(2):
+                cp = psum.tile([P, 4, P], F32, name=f"cp{q}_{i}", tag="cp", bufs=2)
+                for t in range(4):
+                    for g in range(2):
+                        cols = slice((2 * i + g) * P, (2 * i + g + 1) * P)
+                        nc.tensor.matmul_mx(
+                            out=cp[:, t, :],
+                            lhsT=wcq_codes[:, g, t * P : (t + 1) * P].bitcast(FP8X4),
+                            lhsT_scale=wcq_sc[:, g, t * P : (t + 1) * P],
+                            rhs=codes[:, cols].bitcast(FP8X4), rhs_scale=sc[:, cols],
+                            start=(g == 0), stop=(g == 1))
+                cps[q, i] = cp
+
+        def c_copy(q):
+            cg = work.tile([P, 2, 512], BF16, name=f"cg{q}", tag="cg", align_bytes=64)
+            for i in range(2):
+                nc.scalar.copy(out=cg[:, i, :].rearrange("p (n t) -> p n t", t=4),
+                               in_=cps[q, i][:].rearrange("p t n -> p n t"))
+            cgs[q] = cg
+
+        def c_quant(q):
+            c, j = q // 2, q % 2
+            if j == 0:
+                codes = work.tile([P, 512], U32, name=f"cc{c}", tag="cc", align_bytes=64)
+                sc = work.tile([P, 512], U8, name=f"cs{c}", tag="cs", align_bytes=64)
+                ccodes[c] = (codes, sc)
+            codes, sc = ccodes[c]
+            cols = slice(j * 256, (j + 1) * 256)
+            nc.vector.quantize_mx(out=codes[:, cols].bitcast(FP8X4), scales=sc[:, cols],
+                                  in_=cgs[q][:].rearrange("p i k -> p (i k)"))
+
+        def mm2a(q):
+            codes, sc = ccodes[q // 2]
+            for i in range(2):
+                j = 2 * (q % 2) + i
+                ap_ = psum.tile([P, 512], F32, name=f"ap{q}_{i}", tag="ra", bufs=2)
+                nc.tensor.matmul_mx(out=ap_[:], lhsT=codes[:, j * P : (j + 1) * P].bitcast(FP8X4),
+                                    lhsT_scale=sc[:, j * P : (j + 1) * P],
+                                    rhs=wq_codes[:].bitcast(FP8X4), rhs_scale=wq_sc[:], start=True, stop=True)
+                aps[q, i] = ap_
+
+        def a_copy(q):
+            c = q // 2
+            if q % 2 == 0:
+                o = work.tile([P, H, 4, 2 * DH], F32, name=f"o{c}", tag="o", align_bytes=64)
+                osb[c] = o
+            for i in range(2):
+                nc.scalar.copy(out=osb[c][:, :, 2 * (q % 2) + i, 0:DH],
+                               in_=aps[q, i][:].rearrange("p (n d) -> p n d", n=H))
+
+        def mm2u(c, n):
+            codes, sc = ccodes[c]
+            up = psum.tile([P, 512], F32, name=f"up{c}_{n}", tag="up", bufs=2)
+            nc.tensor.matmul_mx(out=up[:], lhsT=wqr_codes[:, n * P : (n + 1) * P].bitcast(FP8X4),
+                                lhsT_scale=wqr_sc[:, n * P : (n + 1) * P],
+                                rhs=codes[:].bitcast(FP8X4), rhs_scale=sc[:], start=True, stop=True)
+            ups[c, n] = up
+
+        def rope_mul(c, n):
+            t = work.tile([P, 2, 512], F32, name=f"t_{c}_{n}", tag="t", bufs=4, align_bytes=64)
+            nc.vector.tensor_tensor(out=t[:], in0=ups[c, n][:].unsqueeze(1).to_broadcast([P, 2, 512]),
+                                    in1=tab[:, c % 2, :, :], op=ALU.mult)
+            ts[c, n] = t
+
+        def r_transpose(c, n):
+            rp = psum.tile([P, 4, P], F32, name=f"rp{c}_{n}", tag="ra", bufs=2)
+            for j in range(4):
+                cols = slice(j * P, (j + 1) * P)
+                nc.tensor.matmul(rp[:, j, :], lhsT=ts[c, n][:, 0, cols], rhs=ident[:], is_transpose=True,
+                                 start=True, stop=False)
+                nc.tensor.matmul(rp[:, j, :], lhsT=ts[c, n][:, 1, cols], rhs=perm[:], is_transpose=True,
+                                 start=False, stop=True)
+            rps[c, n] = rp
+
+        def r_copy(c, n):
+            nc.scalar.copy(out=osb[c][:, n, :, DH : 2 * DH], in_=rps[c, n][:])
+
+        def store(c, n):
+            b, half = c // 2, c % 2
+            nc.sync.dma_start(
+                out=out[b, n, half * 512 : (half + 1) * 512, :].rearrange("(p j) d -> p j d", j=4),
+                in_=osb[c][:, n, :, :])
+
+        def heads(s):
+            return [(s // 2, 2 * (s % 2) + e) for e in range(2)] if 0 <= s < NP else []
+
+        def step(q):
+            if 0 <= q - 2 < NP:
+                c_quant(q - 2)
+            for cn in heads(q - 5):
+                r_transpose(*cn)
+            if q < NP:
+                h_transpose(q)
+            for cn in heads(q - 4):
+                rope_mul(*cn)
+            for cn in heads(q - 5):
+                r_copy(*cn)
+                store(*cn)
+            if q < NP:
+                h_copy(q)
+            widen(q + AHEAD)
+            if q < NP:
+                h_quant(q)
+            if 0 <= q - 1 < NP:
+                mm1(q - 1)
+                c_copy(q - 1)
+            if 0 <= q - 2 < NP:
+                mm2a(q - 2)
+            for cn in heads(q - 3):
+                mm2u(*cn)
+            if 0 <= q - 2 < NP:
+                a_copy(q - 2)
+
+        wcq_copy(nc.scalar.copy, 0)
+        for q in range(AHEAD - 1):
+            widen(q)
+        wcq_copy(nc.scalar.copy, 1)
+        wcq_quant(0)
+        wcq_quant(1)
+        widen(AHEAD - 1)
+        step(0)
+        turns_g()
+        w_copy(nc.scalar.copy, wq_g, wq_raw)
+        step(1)
+        nc.vector.quantize_mx(out=wq_codes[:].bitcast(FP8X4), scales=wq_sc[:], in_=wq_g[:])
+        w_copy(nc.scalar.copy, wqr_g, wqr_raw)
+        tables_v()
+        step(2)
+        tables_s()
+        nc.vector.quantize_mx(out=wqr_codes[:].bitcast(FP8X4), scales=wqr_sc[:], in_=wqr_g[:])
+        for q in range(3, NP + 5):
+            step(q)

@@ -19,7 +19,17 @@ P = 128
 NT = B * S // P
 NC = NT // 4
 NP = NT // 2
-AHEAD = 3
+W0 = 4
+WB = 1
+PQ, PR, PS = 1, 1, -1
+OFF = set()
+RE = False
+HV, CV, AV, RV = (), (), (), ()
+
+
+def WT(q):
+    return int(2 * (q + 2))
+
 
 FLOPS = 2 * B * S * (D * CQ + 2 * CQ * H * DH) + 3 * B * S * H * DH
 
@@ -54,8 +64,8 @@ def tile_mla_pa_t_kernel(tc, h_bytes, h_scale, w_cq, w_q, w_qr, out):
 
         wq_raw = keep.tile([P, 4, H * DH], BF16, name="wq_raw", align_bytes=64)
         wqr_raw = keep.tile([P, 4, H * DH], BF16, name="wqr_raw", align_bytes=64)
-        load_wcq(0)
         load_h(0, 0, 2)
+        load_wcq(0)
         load_wcq(1)
         load_h(0, 2, 4)
         nc.sync.dma_start(out=wq_raw[:], in_=w_q.rearrange("(p j) c -> p j c", j=4))
@@ -84,40 +94,19 @@ def tile_mla_pa_t_kernel(tc, h_bytes, h_scale, w_cq, w_q, w_qr, out):
         s_row = keep.tile([P, S], F32, name="s_row", align_bytes=64)
         nc.gpsimd.iota(s_row[:].rearrange("p (c j q) -> p c j q", c=2, j=4), pattern=[[512, 2], [1, 4], [4, 128]],
                        base=0, channel_multiplier=0, allow_small_or_imprecise_dtypes=True)
-        hpi = keep.tile([P, 1], F32, name="hpi")
-        nc.gpsimd.memset(hpi[:], 1.0)
-        hpi2 = keep.tile([P, 1], F32, name="hpi2")
-        nc.gpsimd.tensor_scalar(out=hpi2[:], in0=hpi[:], scalar1=math.pi / 2, scalar2=None, op0=ALU.mult)
-        perm = keep.tile([P, P], F32, name="perm", align_bytes=64)
-        for e in range(2):
-            nc.gpsimd.tensor_copy(out=perm[:].rearrange("p (i two) -> p two i", two=2)[:, e, :],
-                                  in_=ident[:].rearrange("p (i two) -> p two i", two=2)[:, 1 - e, :])
-
-        scale = keep.tile([P, 2, D], F32, name="scale", align_bytes=64)
-        sc_ps = [psum.tile([P, 4, P], F32, name=f"sc_ps{k}", tag="ht", bufs=2) for k in range(2)]
-        for k in range(8):
-            nc.tensor.transpose(sc_ps[k // 4][:, k % 4, :], sv[:, k : k + 1].to_broadcast([P, P]), ident[:])
-        scv = scale[:].rearrange("p r (q k c) -> p r k q c", k=2, c=4)
-        for r in range(2):
-            nc.vector.tensor_copy(out=scv[:, r, 0], in_=sc_ps[0][:].rearrange("p c q -> p q c"))
-            nc.scalar.copy(out=scv[:, r, 1], in_=sc_ps[1][:].rearrange("p c q -> p q c"))
-
         th_ps = psum.tile([P, P], F32, name="th_ps", tag="ra", bufs=2)
-        thc = keep.tile([P, 1], F32, name="thc")
+        nc.tensor.transpose(th_ps[:], th2[:], ident[:])
         turns = keep.tile([P, S], F32, name="turns", align_bytes=64)
         whole = keep.tile([P, S], I32, name="whole", align_bytes=64)
         frac = keep.tile([P, S], F32, name="frac", align_bytes=64)
         fabs = keep.tile([P, S], F32, name="fabs", align_bytes=64)
         tab = keep.tile([P, 2, 2, 512], F32, name="tab", align_bytes=64)
-
-        def turns_g():
-            nc.tensor.transpose(th_ps[:], th2[:], ident[:])
-            nc.scalar.copy(out=thc[:], in_=th_ps[:, 0:1])
-            nc.gpsimd.tensor_scalar(out=turns[:], in0=s_row[:], scalar1=thc[:, 0:1], scalar2=0.0,
-                                    op0=ALU.mult, op1=ALU.add)
+        thc = keep.tile([P, 1], F32, name="thc")
+        nc.vector.tensor_copy(out=thc[:], in_=th_ps[:, 0:1])
+        nc.vector.tensor_scalar(out=turns[:], in0=s_row[:], scalar1=thc[:, 0:1], scalar2=None, op0=ALU.mult)
+        nc.vector.tensor_copy(out=whole[:], in_=turns[:])
 
         def tables_v():
-            nc.vector.tensor_copy(out=whole[:], in_=turns[:])
             nc.vector.tensor_tensor(out=frac[:], in0=turns[:], in1=whole[:], op=ALU.subtract)
 
         def tables_s():
@@ -126,6 +115,15 @@ def tile_mla_pa_t_kernel(tc, h_bytes, h_scale, w_cq, w_q, w_qr, out):
             nc.scalar.activation(out=tab[:, :, 1, :], in_=fr, func=ACT.Sin, scale=2.0 * math.pi)
             nc.scalar.activation(out=fa, in_=fr, func=ACT.Abs)
             nc.scalar.activation(out=tab[:, :, 0, :], in_=fa, func=ACT.Sin, scale=-2.0 * math.pi, bias=hpi2[:, 0:1])
+
+        hpi = keep.tile([P, 1], F32, name="hpi")
+        nc.gpsimd.memset(hpi[:], 1.0)
+        hpi2 = keep.tile([P, 1], F32, name="hpi2")
+        nc.gpsimd.tensor_scalar(out=hpi2[:], in0=hpi[:], scalar1=math.pi / 2, scalar2=None, op0=ALU.mult)
+        perm = keep.tile([P, P], F32, name="perm", align_bytes=64)
+        for e in range(2):
+            nc.gpsimd.tensor_copy(out=perm[:].rearrange("p (i two) -> p two i", two=2)[:, e, :],
+                                  in_=ident[:].rearrange("p (i two) -> p two i", two=2)[:, 1 - e, :])
 
         wcq_codes = keep.tile([P, 2, CQ], U32, name="wcq_codes", align_bytes=64)
         wcq_sc = keep.tile([P, 2, CQ], U8, name="wcq_sc", align_bytes=64)
@@ -147,20 +145,31 @@ def tile_mla_pa_t_kernel(tc, h_bytes, h_scale, w_cq, w_q, w_qr, out):
         def w_copy(copy, grouped, raw):
             copy(out=grouped[:].rearrange("p (n j) -> p n j", j=4), in_=raw[:].rearrange("p j n -> p n j"))
 
+        scale = keep.tile([P, D], F32, name="scale", align_bytes=64)
+        sc_ps = [psum.tile([P, 4, P], F32, name=f"sc_ps{k}", tag="ht", bufs=2) for k in range(2)]
+        for k in range(8):
+            nc.tensor.transpose(sc_ps[k // 4][:, k % 4, :], sv[:, k : k + 1].to_broadcast([P, P]), ident[:])
+        scv = scale[:].rearrange("p (q k c) -> p k q c", k=2, c=4)
+        nc.vector.tensor_copy(out=scv[:, 0], in_=sc_ps[0][:].rearrange("p c q -> p q c"))
+        nc.scalar.copy(out=scv[:, 1], in_=sc_ps[1][:].rearrange("p c q -> p q c"))
+        tables_v()
+
+        V = nc.vector.tensor_copy
+        A = nc.scalar.copy
+
         xb, hps, grp, hq, cps, cgs, ccodes, ups, ts, rps, aps, osb = ({} for k in range(12))
 
-        def widen(q):
-            if not 0 <= q < NP:
-                return
-            j = 2 * (q % 2)
-            x = work.tile([P, 2, D], BF16, name=f"x{q}", tag="x", bufs=AHEAD + 2, align_bytes=64)
-            nc.vector.tensor_tensor(out=x[:], in0=hb[q // 2][:, j : j + 2, :].bitcast(E4M3), in1=scale[:], op=ALU.mult)
-            xb[q] = x
+        def widen_to(n):
+            while len(xb) < min(n, NT):
+                i = len(xb)
+                x = work.tile([P, D], BF16, name=f"x{i}", tag="x", bufs=12, align_bytes=64)
+                nc.vector.tensor_tensor(out=x[:], in0=hb[i // 4][:, i % 4, :].bitcast(E4M3), in1=scale[:], op=ALU.mult)
+                xb[i] = x
 
         def h_transpose(q):
             for i in range(2):
                 ht = psum.tile([P, 2, 2, P], F32, name=f"ht{q}_{i}", tag="ht", bufs=2)
-                words = xb[q][:, i, :].bitcast(F32)
+                words = xb[2 * q + i][:].bitcast(F32)
                 for g in range(2):
                     for u in range(2):
                         nc.tensor.transpose(ht[:, g, u, :], words[:, 256 * g + u : 256 * (g + 1) : 2], ident[:])
@@ -169,7 +178,7 @@ def tile_mla_pa_t_kernel(tc, h_bytes, h_scale, w_cq, w_q, w_qr, out):
         def h_copy(q):
             gt = work.tile([P, 2, D], BF16, name=f"g{q}", tag="g", align_bytes=64)
             for i in range(2):
-                nc.scalar.copy(out=gt[:, i, :].bitcast(F32).rearrange("p (g n u) -> p g n u", g=2, u=2),
+                (V if (i == 1 and q in HV) else A)(out=gt[:, i, :].bitcast(F32).rearrange("p (g n u) -> p g n u", g=2, u=2),
                                in_=hps[q, i][:].rearrange("p g u n -> p g n u"))
             grp[q] = gt
 
@@ -198,28 +207,23 @@ def tile_mla_pa_t_kernel(tc, h_bytes, h_scale, w_cq, w_q, w_qr, out):
         def c_copy(q):
             cg = work.tile([P, 2, 512], BF16, name=f"cg{q}", tag="cg", align_bytes=64)
             for i in range(2):
-                nc.scalar.copy(out=cg[:, i, :].rearrange("p (n t) -> p n t", t=4),
+                (V if (i == 1 and q in CV) else A)(out=cg[:, i, :].rearrange("p (n t) -> p n t", t=4),
                                in_=cps[q, i][:].rearrange("p t n -> p n t"))
             cgs[q] = cg
 
         def c_quant(q):
-            c, j = q // 2, q % 2
-            if j == 0:
-                codes = work.tile([P, 512], U32, name=f"cc{c}", tag="cc", align_bytes=64)
-                sc = work.tile([P, 512], U8, name=f"cs{c}", tag="cs", align_bytes=64)
-                ccodes[c] = (codes, sc)
-            codes, sc = ccodes[c]
-            cols = slice(j * 256, (j + 1) * 256)
-            nc.vector.quantize_mx(out=codes[:, cols].bitcast(FP8X4), scales=sc[:, cols],
+            codes = work.tile([P, 256], U32, name=f"cc{q}", tag="cc", align_bytes=64)
+            sc = work.tile([P, 256], U8, name=f"cs{q}", tag="cs", align_bytes=64)
+            nc.vector.quantize_mx(out=codes[:].bitcast(FP8X4), scales=sc[:],
                                   in_=cgs[q][:].rearrange("p i k -> p (i k)"))
+            ccodes[q] = (codes, sc)
 
         def mm2a(q):
-            codes, sc = ccodes[q // 2]
+            codes, sc = ccodes[q]
             for i in range(2):
-                j = 2 * (q % 2) + i
                 ap_ = psum.tile([P, 512], F32, name=f"ap{q}_{i}", tag="ra", bufs=2)
-                nc.tensor.matmul_mx(out=ap_[:], lhsT=codes[:, j * P : (j + 1) * P].bitcast(FP8X4),
-                                    lhsT_scale=sc[:, j * P : (j + 1) * P],
+                nc.tensor.matmul_mx(out=ap_[:], lhsT=codes[:, i * P : (i + 1) * P].bitcast(FP8X4),
+                                    lhsT_scale=sc[:, i * P : (i + 1) * P],
                                     rhs=wq_codes[:].bitcast(FP8X4), rhs_scale=wq_sc[:], start=True, stop=True)
                 aps[q, i] = ap_
 
@@ -229,88 +233,127 @@ def tile_mla_pa_t_kernel(tc, h_bytes, h_scale, w_cq, w_q, w_qr, out):
                 o = work.tile([P, H, 4, 2 * DH], F32, name=f"o{c}", tag="o", align_bytes=64)
                 osb[c] = o
             for i in range(2):
-                nc.scalar.copy(out=osb[c][:, :, 2 * (q % 2) + i, 0:DH],
+                (V if (i == 1 and q in AV) else A)(out=osb[c][:, :, 2 * (q % 2) + i, 0:DH],
                                in_=aps[q, i][:].rearrange("p (n d) -> p n d", n=H))
 
-        def mm2u(c, n):
-            codes, sc = ccodes[c]
-            up = psum.tile([P, 512], F32, name=f"up{c}_{n}", tag="up", bufs=2)
-            nc.tensor.matmul_mx(out=up[:], lhsT=wqr_codes[:, n * P : (n + 1) * P].bitcast(FP8X4),
-                                lhsT_scale=wqr_sc[:, n * P : (n + 1) * P],
-                                rhs=codes[:].bitcast(FP8X4), rhs_scale=sc[:], start=True, stop=True)
-            ups[c, n] = up
+        def mm2u(q, y):
+            codes, sc = ccodes[q]
+            up = psum.tile([P, 2, 256], F32, name=f"up{q}_{y}", tag="up", bufs=2)
+            for e in range(2):
+                n = 2 * y + e
+                nc.tensor.matmul_mx(out=up[:, e, :], lhsT=wqr_codes[:, n * P : (n + 1) * P].bitcast(FP8X4),
+                                    lhsT_scale=wqr_sc[:, n * P : (n + 1) * P],
+                                    rhs=codes[:].bitcast(FP8X4), rhs_scale=sc[:], start=True, stop=True)
+            ups[q, y] = up
 
-        def rope_mul(c, n):
-            t = work.tile([P, 2, 512], F32, name=f"t_{c}_{n}", tag="t", bufs=4, align_bytes=64)
-            nc.vector.tensor_tensor(out=t[:], in0=ups[c, n][:].unsqueeze(1).to_broadcast([P, 2, 512]),
-                                    in1=tab[:, c % 2, :, :], op=ALU.mult)
-            ts[c, n] = t
+        usb = {}
 
-        def r_transpose(c, n):
-            rp = psum.tile([P, 4, P], F32, name=f"rp{c}_{n}", tag="ra", bufs=2)
-            for j in range(4):
-                cols = slice(j * P, (j + 1) * P)
-                nc.tensor.matmul(rp[:, j, :], lhsT=ts[c, n][:, 0, cols], rhs=ident[:], is_transpose=True,
-                                 start=True, stop=False)
-                nc.tensor.matmul(rp[:, j, :], lhsT=ts[c, n][:, 1, cols], rhs=perm[:], is_transpose=True,
-                                 start=False, stop=True)
-            rps[c, n] = rp
+        def u_copy(q, y):
+            us = work.tile([P, 2, 256], F32, name=f"us{q}_{y}", tag="us", align_bytes=64)
+            nc.scalar.copy(out=us[:], in_=ups[q, y][:])
+            usb[q, y] = us
 
-        def r_copy(c, n):
-            nc.scalar.copy(out=osb[c][:, n, :, DH : 2 * DH], in_=rps[c, n][:])
+        def rope_mul(q, y):
+            t = work.tile([P, 2, 2, 256], F32, name=f"t{q}_{y}", tag="t", bufs=4, align_bytes=64)
+            k = q % 4
+            cs = tab[:, k // 2, :, 256 * (k % 2) : 256 * (k % 2 + 1)]
+            if (q, y) in usb:
+                nc.gpsimd.tensor_tensor(out=t[:, 1], in0=usb[q, y][:],
+                                        in1=cs[:, 1, :].unsqueeze(1).to_broadcast([P, 2, 256]), op=ALU.mult)
+                nc.vector.tensor_tensor(out=t[:, 0], in0=ups[q, y][:],
+                                        in1=cs[:, 0, :].unsqueeze(1).to_broadcast([P, 2, 256]), op=ALU.mult)
+            else:
+                nc.vector.tensor_tensor(out=t[:], in0=ups[q, y][:].unsqueeze(1).to_broadcast([P, 2, 2, 256]),
+                                        in1=cs.unsqueeze(2).to_broadcast([P, 2, 2, 256]), op=ALU.mult)
+            ts[q, y] = t
 
-        def store(c, n):
+        def r_transpose(q, y):
+            rp = psum.tile([P, 2, 2, P], F32, name=f"rp{q}_{y}", tag="ra", bufs=2)
+            for e in range(2):
+                for i in range(2):
+                    cols = slice(i * P, (i + 1) * P)
+                    nc.tensor.matmul(rp[:, e, i, :], lhsT=ts[q, y][:, 0, e, cols], rhs=ident[:], is_transpose=True,
+                                     start=True, stop=False)
+                    nc.tensor.matmul(rp[:, e, i, :], lhsT=ts[q, y][:, 1, e, cols], rhs=perm[:], is_transpose=True,
+                                     start=False, stop=True)
+            rps[q, y] = rp
+
+        def r_copy(q, y):
+            c, j = q // 2, 2 * (q % 2)
+            (V if (y == 1 and q in RV) else A)(out=osb[c][:, 2 * y : 2 * y + 2, j : j + 2, DH : 2 * DH], in_=rps[q, y][:])
+
+        def store(q, y):
+            c = q // 2
+            j0, j1 = 2 * (q % 2), 2 * (q % 2) + 2
             b, half = c // 2, c % 2
-            nc.sync.dma_start(
-                out=out[b, n, half * 512 : (half + 1) * 512, :].rearrange("(p j) d -> p j d", j=4),
-                in_=osb[c][:, n, :, :])
+            for n in (2 * y, 2 * y + 1):
+                nc.sync.dma_start(
+                    out=out[b, n, half * 512 : (half + 1) * 512, :].rearrange("(p j) d -> p j d", j=4)[:, j0:j1, :],
+                    in_=osb[c][:, n, j0:j1, :])
 
-        def heads(s):
-            return [(s // 2, 2 * (s % 2) + e) for e in range(2)] if 0 <= s < NP else []
+        def units(q):
+            return [(q, 0), (q, 1)] if 0 <= q < NP else []
+
+        def rope_end(q):
+            for un in units(q):
+                r_transpose(*un)
+            for un in units(q):
+                r_copy(*un)
+                store(*un)
 
         def step(q):
-            if 0 <= q - 2 < NP:
-                c_quant(q - 2)
-            for cn in heads(q - 5):
-                r_transpose(*cn)
             if q < NP:
                 h_transpose(q)
-            for cn in heads(q - 4):
-                rope_mul(*cn)
-            for cn in heads(q - 5):
-                r_copy(*cn)
-                store(*cn)
-            if q < NP:
                 h_copy(q)
-            widen(q + AHEAD)
-            if q < NP:
-                h_quant(q)
             if 0 <= q - 1 < NP:
                 mm1(q - 1)
+            for un in units(q - 2):
+                if un in OFF:
+                    u_copy(*un)
+            for un in units(q - 2):
+                rope_mul(*un)
+            if 0 <= q - 1 < NP:
                 c_copy(q - 1)
-            if 0 <= q - 2 < NP:
-                mm2a(q - 2)
-            for cn in heads(q - 3):
-                mm2u(*cn)
-            if 0 <= q - 2 < NP:
-                a_copy(q - 2)
+            for un in units(q - 3):
+                r_transpose(*un)
+            for un in units(q - 3):
+                r_copy(*un)
+                store(*un)
+            widen_to(WT(q) - WB)
+            if 0 <= q - 1 < NP:
+                c_quant(q - 1)
+            widen_to(WT(q))
+            if q < NP:
+                h_quant(q)
+            for un in units(q - 1):
+                mm2u(*un)
+            if q == NP and RE:
+                rope_end(q - 2)
+            if 0 <= q - 1 < NP:
+                mm2a(q - 1)
+                a_copy(q - 1)
 
-        wcq_copy(nc.scalar.copy, 0)
-        for q in range(AHEAD - 1):
-            widen(q)
-        wcq_copy(nc.scalar.copy, 1)
+        if PS < 0:
+            tables_s()
+        widen_to(2)
+        wcq_copy(V, 0)
+        wcq_copy(V, 1)
         wcq_quant(0)
         wcq_quant(1)
-        widen(AHEAD - 1)
-        step(0)
-        turns_g()
-        w_copy(nc.scalar.copy, wq_g, wq_raw)
-        step(1)
-        nc.vector.quantize_mx(out=wq_codes[:].bitcast(FP8X4), scales=wq_sc[:], in_=wq_g[:])
-        w_copy(nc.scalar.copy, wqr_g, wqr_raw)
-        tables_v()
-        step(2)
-        tables_s()
-        nc.vector.quantize_mx(out=wqr_codes[:].bitcast(FP8X4), scales=wqr_sc[:], in_=wqr_g[:])
-        for q in range(3, NP + 5):
+        widen_to(W0)
+        for q in range(0, NP + 1):
+            if q == PQ:
+                w_copy(A, wq_g, wq_raw)
+            if q == PR:
+                w_copy(A, wqr_g, wqr_raw)
+            if q == PS:
+                tables_s()
+            if q == 1:
+                nc.vector.quantize_mx(out=wq_codes[:].bitcast(FP8X4), scales=wq_sc[:], in_=wq_g[:])
+                nc.vector.quantize_mx(out=wqr_codes[:].bitcast(FP8X4), scales=wqr_sc[:], in_=wqr_g[:])
             step(q)
+        if not RE:
+            rope_end(NP - 2)
+        for un in units(NP - 1):
+            rope_mul(*un)
+        rope_end(NP - 1)

@@ -18,17 +18,10 @@ B, S, D, H, DH, CQ = 4, 1024, 1024, 4, 128, 512
 P = 128
 NT = B * S // P
 NC = NT // 4
-NP = NT // 2
-W0 = 4
-WB = 1
-PQ, PR, PS = 1, 1, -1
-OFF = set()
-RE = False
-HV, CV, AV, RV = (), (), (), ()
 
 
-def WT(q):
-    return int(2 * (q + 2))
+def WT(s):
+    return s + 3
 
 
 FLOPS = 2 * B * S * (D * CQ + 2 * CQ * H * DH) + 3 * B * S * H * DH
@@ -36,42 +29,39 @@ FLOPS = 2 * B * S * (D * CQ + 2 * CQ * H * DH) + 3 * B * S * H * DH
 
 def tile_mla_pa_t_kernel(tc, h_bytes, h_scale, w_cq, w_q, w_qr, out):
     nc = tc.nc
+    V = nc.vector.tensor_copy
+    A = nc.scalar.copy
     with ExitStack() as ctx:
         keep = ctx.enter_context(tc.tile_pool(name="keep", bufs=1))
         work = ctx.enter_context(tc.tile_pool(name="work", bufs=3))
-        psum = ctx.enter_context(tc.psum_pool(name="psum", bufs=1))
+        psum = ctx.enter_context(tc.psum_pool(name="psum", bufs=2))
         ctx.enter_context(tc.manual_schedule())
 
-        hb = []
-        for c in range(NC):
-            t = keep.tile([P, 4, D], U8, name=f"hb{c}", align_bytes=64)
-            hb.append(t)
+        hb = [keep.tile([P, 4, D], U8, name=f"hb{c}", align_bytes=64) for c in range(NC)]
 
         def load_h(c, j0, j1):
             b, half = c // 2, c % 2
             nc.sync.dma_start(
                 out=hb[c][:, j0:j1, :],
-                in_=h_bytes[b, half * 512 : (half + 1) * 512, :].rearrange("(p j) k -> p j k", j=4)[:, j0:j1, :],
-            )
+                in_=h_bytes[b, half * 512 : (half + 1) * 512, :].rearrange("(p j) k -> p j k", j=4)[:, j0:j1, :])
 
         sv = keep.tile([P, 8], F32, name="sv")
         nc.sync.dma_start(out=sv[:], in_=h_scale.rearrange("a b (p c) -> p (a b c)", c=8))
         wcq_raw = [keep.tile([P, 4, CQ], BF16, name=f"wcq_raw{g}", align_bytes=64) for g in range(2)]
+        wq_raw = keep.tile([P, 4, H * DH], BF16, name="wq_raw", align_bytes=64)
+        wqr_raw = keep.tile([P, 4, H * DH], BF16, name="wqr_raw", align_bytes=64)
 
         def load_wcq(g):
             nc.sync.dma_start(out=wcq_raw[g][:],
                               in_=w_cq[g * 512 : (g + 1) * 512, :].rearrange("(p j) c -> p j c", j=4))
 
-        wq_raw = keep.tile([P, 4, H * DH], BF16, name="wq_raw", align_bytes=64)
-        wqr_raw = keep.tile([P, 4, H * DH], BF16, name="wqr_raw", align_bytes=64)
         load_h(0, 0, 2)
         load_wcq(0)
         load_wcq(1)
         load_h(0, 2, 4)
-        nc.sync.dma_start(out=wq_raw[:], in_=w_q.rearrange("(p j) c -> p j c", j=4))
-        load_h(1, 0, 4)
         nc.sync.dma_start(out=wqr_raw[:], in_=w_qr.rearrange("(p j) c -> p j c", j=4))
-        for c in range(2, NC):
+        nc.sync.dma_start(out=wq_raw[:], in_=w_q.rearrange("(p j) c -> p j c", j=4))
+        for c in range(1, NC):
             load_h(c, 0, 4)
 
         ident = keep.tile([P, P], F32, name="ident", align_bytes=64)
@@ -80,42 +70,20 @@ def tile_mla_pa_t_kernel(tc, h_bytes, h_scale, w_cq, w_q, w_qr, out):
         nc.gpsimd.memset(warm[:], 0.0)
         warm2 = keep.tile([P, 1], F32, name="warm2")
         nc.scalar.activation(out=warm2[:], in_=warm[:], func=ACT.Sin)
+        s_row = keep.tile([P, S], F32, name="s_row", align_bytes=64)
+        nc.gpsimd.iota(s_row[:].rearrange("p (c j q) -> p c j q", c=2, j=4), pattern=[[512, 2], [1, 4], [4, 128]],
+                       base=0, channel_multiplier=0, allow_small_or_imprecise_dtypes=True)
         th = keep.tile([P, 64], F32, name="th")
-        nc.gpsimd.memset(th[:, 0:1], 1.0)
+        nc.vector.memset(th[:, 0:1], 1.0)
         w = 1
         while w < 64:
-            nc.gpsimd.tensor_scalar(out=th[:, w : 2 * w], in0=th[:, 0:w], scalar1=10000.0 ** (-w / 64.0),
+            nc.vector.tensor_scalar(out=th[:, w : 2 * w], in0=th[:, 0:w], scalar1=10000.0 ** (-w / 64.0),
                                     scalar2=None, op0=ALU.mult)
             w *= 2
         th2 = keep.tile([P, P], F32, name="th2", align_bytes=64)
         for e in range(2):
-            nc.gpsimd.tensor_scalar(out=th2[:].rearrange("p (i two) -> p two i", two=2)[:, e, :], in0=th[:],
+            nc.vector.tensor_scalar(out=th2[:].rearrange("p (i two) -> p two i", two=2)[:, e, :], in0=th[:],
                                     scalar1=(1.0 - 2.0 * e) / (2.0 * math.pi), scalar2=None, op0=ALU.mult)
-        s_row = keep.tile([P, S], F32, name="s_row", align_bytes=64)
-        nc.gpsimd.iota(s_row[:].rearrange("p (c j q) -> p c j q", c=2, j=4), pattern=[[512, 2], [1, 4], [4, 128]],
-                       base=0, channel_multiplier=0, allow_small_or_imprecise_dtypes=True)
-        th_ps = psum.tile([P, P], F32, name="th_ps", tag="ra", bufs=2)
-        nc.tensor.transpose(th_ps[:], th2[:], ident[:])
-        turns = keep.tile([P, S], F32, name="turns", align_bytes=64)
-        whole = keep.tile([P, S], I32, name="whole", align_bytes=64)
-        frac = keep.tile([P, S], F32, name="frac", align_bytes=64)
-        fabs = keep.tile([P, S], F32, name="fabs", align_bytes=64)
-        tab = keep.tile([P, 2, 2, 512], F32, name="tab", align_bytes=64)
-        thc = keep.tile([P, 1], F32, name="thc")
-        nc.vector.tensor_copy(out=thc[:], in_=th_ps[:, 0:1])
-        nc.vector.tensor_scalar(out=turns[:], in0=s_row[:], scalar1=thc[:, 0:1], scalar2=None, op0=ALU.mult)
-        nc.vector.tensor_copy(out=whole[:], in_=turns[:])
-
-        def tables_v():
-            nc.vector.tensor_tensor(out=frac[:], in0=turns[:], in1=whole[:], op=ALU.subtract)
-
-        def tables_s():
-            fr = frac[:].rearrange("p (h q) -> p h q", h=2)
-            fa = fabs[:].rearrange("p (h q) -> p h q", h=2)
-            nc.scalar.activation(out=tab[:, :, 1, :], in_=fr, func=ACT.Sin, scale=2.0 * math.pi)
-            nc.scalar.activation(out=fa, in_=fr, func=ACT.Abs)
-            nc.scalar.activation(out=tab[:, :, 0, :], in_=fa, func=ACT.Sin, scale=-2.0 * math.pi, bias=hpi2[:, 0:1])
-
         hpi = keep.tile([P, 1], F32, name="hpi")
         nc.gpsimd.memset(hpi[:], 1.0)
         hpi2 = keep.tile([P, 1], F32, name="hpi2")
@@ -124,6 +92,43 @@ def tile_mla_pa_t_kernel(tc, h_bytes, h_scale, w_cq, w_q, w_qr, out):
         for e in range(2):
             nc.gpsimd.tensor_copy(out=perm[:].rearrange("p (i two) -> p two i", two=2)[:, e, :],
                                   in_=ident[:].rearrange("p (i two) -> p two i", two=2)[:, 1 - e, :])
+        th_ps = psum.tile([P, P], F32, name="th_ps", tag="ra")
+        nc.tensor.transpose(th_ps[:], th2[:], ident[:])
+
+        scale = keep.tile([P, D], F32, name="scale", align_bytes=64)
+        sc_ps = [psum.tile([P, 4, P], F32, name=f"sc_ps{k}", tag="ht") for k in range(2)]
+        for k in range(8):
+            nc.tensor.transpose(sc_ps[k // 4][:, k % 4, :], sv[:, k : k + 1].to_broadcast([P, P]), ident[:])
+        scv = scale[:].rearrange("p (q k c) -> p k q c", k=2, c=4)
+        nc.scalar.copy(out=scv[:, 1], in_=sc_ps[1][:].rearrange("p c q -> p q c"))
+        thc = keep.tile([P, 1], F32, name="thc")
+        nc.vector.tensor_copy(out=thc[:], in_=th_ps[:, 0:1])
+        nc.vector.tensor_copy(out=scv[:, 0], in_=sc_ps[0][:].rearrange("p c q -> p q c"))
+
+        turns = keep.tile([P, S], F32, name="turns", align_bytes=64)
+        whole = keep.tile([P, S], I32, name="whole", align_bytes=64)
+        frac = keep.tile([P, S], F32, name="frac", align_bytes=64)
+        fabs = keep.tile([P, S], F32, name="fabs", align_bytes=64)
+        tab = keep.tile([P, 2, 2, 512], F32, name="tab", align_bytes=64)
+
+        def turns_v(h):
+            cols = slice(512 * h, 512 * (h + 1))
+            nc.vector.tensor_scalar(out=turns[:, cols], in0=s_row[:, cols], scalar1=thc[:, 0:1], scalar2=None,
+                                    op0=ALU.mult)
+        def whole_v(h):
+            cols = slice(512 * h, 512 * (h + 1))
+            nc.vector.tensor_copy(out=whole[:, cols], in_=turns[:, cols])
+
+        def frac_v(h):
+            cols = slice(512 * h, 512 * (h + 1))
+            nc.vector.tensor_tensor(out=frac[:, cols], in0=turns[:, cols], in1=whole[:, cols], op=ALU.subtract)
+
+        def tables_s(h):
+            cols = slice(512 * h, 512 * (h + 1))
+            nc.scalar.activation(out=tab[:, h, 1, :], in_=frac[:, cols], func=ACT.Sin, scale=2.0 * math.pi)
+            nc.scalar.activation(out=fabs[:, cols], in_=frac[:, cols], func=ACT.Abs)
+            nc.scalar.activation(out=tab[:, h, 0, :], in_=fabs[:, cols], func=ACT.Sin, scale=-2.0 * math.pi,
+                                 bias=hpi2[:, 0:1])
 
         wcq_codes = keep.tile([P, 2, CQ], U32, name="wcq_codes", align_bytes=64)
         wcq_sc = keep.tile([P, 2, CQ], U8, name="wcq_sc", align_bytes=64)
@@ -145,215 +150,178 @@ def tile_mla_pa_t_kernel(tc, h_bytes, h_scale, w_cq, w_q, w_qr, out):
         def w_copy(copy, grouped, raw):
             copy(out=grouped[:].rearrange("p (n j) -> p n j", j=4), in_=raw[:].rearrange("p j n -> p n j"))
 
-        scale = keep.tile([P, D], F32, name="scale", align_bytes=64)
-        sc_ps = [psum.tile([P, 4, P], F32, name=f"sc_ps{k}", tag="ht", bufs=2) for k in range(2)]
-        for k in range(8):
-            nc.tensor.transpose(sc_ps[k // 4][:, k % 4, :], sv[:, k : k + 1].to_broadcast([P, P]), ident[:])
-        scv = scale[:].rearrange("p (q k c) -> p k q c", k=2, c=4)
-        nc.vector.tensor_copy(out=scv[:, 0], in_=sc_ps[0][:].rearrange("p c q -> p q c"))
-        nc.scalar.copy(out=scv[:, 1], in_=sc_ps[1][:].rearrange("p c q -> p q c"))
-        tables_v()
-
-        V = nc.vector.tensor_copy
-        A = nc.scalar.copy
-
-        xb, hps, grp, hq, cps, cgs, ccodes, ups, ts, rps, aps, osb = ({} for k in range(12))
+        xb, hps, grp, hq, cps, cgs, cq, ups, ts, rps, aps, osb = ({} for k in range(12))
 
         def widen_to(n):
             while len(xb) < min(n, NT):
                 i = len(xb)
-                x = work.tile([P, D], BF16, name=f"x{i}", tag="x", bufs=12, align_bytes=64)
+                x = work.tile([P, D], BF16, name=f"x{i}", tag="x", bufs=8, align_bytes=64)
                 nc.vector.tensor_tensor(out=x[:], in0=hb[i // 4][:, i % 4, :].bitcast(E4M3), in1=scale[:], op=ALU.mult)
                 xb[i] = x
 
-        def h_transpose(q):
-            for i in range(2):
-                ht = psum.tile([P, 2, 2, P], F32, name=f"ht{q}_{i}", tag="ht", bufs=2)
-                words = xb[2 * q + i][:].bitcast(F32)
+        def h_transpose(i):
+            ht = psum.tile([P, 2, 2, P], F32, name=f"ht{i}", tag="ht")
+            words = xb[i][:].bitcast(F32)
+            for g in range(2):
+                for u in range(2):
+                    nc.tensor.transpose(ht[:, g, u, :], words[:, 256 * g + u : 256 * (g + 1) : 2], ident[:])
+            hps[i] = ht
+
+        def h_copy(i):
+            gt = work.tile([P, D], BF16, name=f"g{i}", tag="g", align_bytes=64)
+            nc.scalar.copy(out=gt[:].bitcast(F32).rearrange("p (g n u) -> p g n u", g=2, u=2),
+                           in_=hps[i][:].rearrange("p g u n -> p g n u"))
+            grp[i] = gt
+
+        def h_quant(i):
+            codes = work.tile([P, 256], U32, name=f"hc{i}", tag="hc", align_bytes=64)
+            sc = work.tile([P, 256], U8, name=f"hs{i}", tag="hs", align_bytes=64)
+            nc.vector.quantize_mx(out=codes[:].bitcast(FP8X4), scales=sc[:], in_=grp[i][:])
+            hq[i] = (codes, sc)
+
+        def mm1(i):
+            codes, sc = hq[i]
+            cp = psum.tile([P, 4, P], F32, name=f"cp{i}", tag="cp")
+            for t in range(4):
                 for g in range(2):
-                    for u in range(2):
-                        nc.tensor.transpose(ht[:, g, u, :], words[:, 256 * g + u : 256 * (g + 1) : 2], ident[:])
-                hps[q, i] = ht
+                    cols = slice(g * P, (g + 1) * P)
+                    nc.tensor.matmul_mx(
+                        out=cp[:, t, :],
+                        lhsT=wcq_codes[:, g, t * P : (t + 1) * P].bitcast(FP8X4),
+                        lhsT_scale=wcq_sc[:, g, t * P : (t + 1) * P],
+                        rhs=codes[:, cols].bitcast(FP8X4), rhs_scale=sc[:, cols],
+                        start=(g == 0), stop=(g == 1))
+            cps[i] = cp
 
-        def h_copy(q):
-            gt = work.tile([P, 2, D], BF16, name=f"g{q}", tag="g", align_bytes=64)
-            for i in range(2):
-                (V if (i == 1 and q in HV) else A)(out=gt[:, i, :].bitcast(F32).rearrange("p (g n u) -> p g n u", g=2, u=2),
-                               in_=hps[q, i][:].rearrange("p g u n -> p g n u"))
-            grp[q] = gt
+        def c_copy(i):
+            cg = work.tile([P, 512], BF16, name=f"cg{i}", tag="cg", align_bytes=64)
+            nc.scalar.copy(out=cg[:].rearrange("p (n t) -> p n t", t=4), in_=cps[i][:].rearrange("p t n -> p n t"))
+            cgs[i] = cg
 
-        def h_quant(q):
-            codes = work.tile([P, 512], U32, name=f"hc{q}", tag="hc", align_bytes=64)
-            sc = work.tile([P, 512], U8, name=f"hs{q}", tag="hs", align_bytes=64)
-            nc.vector.quantize_mx(out=codes[:].bitcast(FP8X4), scales=sc[:],
-                                  in_=grp[q][:].rearrange("p i k -> p (i k)"))
-            hq[q] = (codes, sc)
+        def c_quant(i):
+            codes = work.tile([P, P], U32, name=f"cc{i}", tag="cc", align_bytes=64)
+            sc = work.tile([P, P], U8, name=f"cs{i}", tag="cs", align_bytes=64)
+            nc.vector.quantize_mx(out=codes[:].bitcast(FP8X4), scales=sc[:], in_=cgs[i][:])
+            cq[i] = (codes, sc)
 
-        def mm1(q):
-            codes, sc = hq[q]
-            for i in range(2):
-                cp = psum.tile([P, 4, P], F32, name=f"cp{q}_{i}", tag="cp", bufs=2)
-                for t in range(4):
-                    for g in range(2):
-                        cols = slice((2 * i + g) * P, (2 * i + g + 1) * P)
-                        nc.tensor.matmul_mx(
-                            out=cp[:, t, :],
-                            lhsT=wcq_codes[:, g, t * P : (t + 1) * P].bitcast(FP8X4),
-                            lhsT_scale=wcq_sc[:, g, t * P : (t + 1) * P],
-                            rhs=codes[:, cols].bitcast(FP8X4), rhs_scale=sc[:, cols],
-                            start=(g == 0), stop=(g == 1))
-                cps[q, i] = cp
-
-        def c_copy(q):
-            cg = work.tile([P, 2, 512], BF16, name=f"cg{q}", tag="cg", align_bytes=64)
-            for i in range(2):
-                (V if (i == 1 and q in CV) else A)(out=cg[:, i, :].rearrange("p (n t) -> p n t", t=4),
-                               in_=cps[q, i][:].rearrange("p t n -> p n t"))
-            cgs[q] = cg
-
-        def c_quant(q):
-            codes = work.tile([P, 256], U32, name=f"cc{q}", tag="cc", align_bytes=64)
-            sc = work.tile([P, 256], U8, name=f"cs{q}", tag="cs", align_bytes=64)
-            nc.vector.quantize_mx(out=codes[:].bitcast(FP8X4), scales=sc[:],
-                                  in_=cgs[q][:].rearrange("p i k -> p (i k)"))
-            ccodes[q] = (codes, sc)
-
-        def mm2a(q):
-            codes, sc = ccodes[q]
-            for i in range(2):
-                ap_ = psum.tile([P, 512], F32, name=f"ap{q}_{i}", tag="ra", bufs=2)
-                nc.tensor.matmul_mx(out=ap_[:], lhsT=codes[:, i * P : (i + 1) * P].bitcast(FP8X4),
-                                    lhsT_scale=sc[:, i * P : (i + 1) * P],
-                                    rhs=wq_codes[:].bitcast(FP8X4), rhs_scale=wq_sc[:], start=True, stop=True)
-                aps[q, i] = ap_
-
-        def a_copy(q):
-            c = q // 2
-            if q % 2 == 0:
-                o = work.tile([P, H, 4, 2 * DH], F32, name=f"o{c}", tag="o", align_bytes=64)
-                osb[c] = o
-            for i in range(2):
-                (V if (i == 1 and q in AV) else A)(out=osb[c][:, :, 2 * (q % 2) + i, 0:DH],
-                               in_=aps[q, i][:].rearrange("p (n d) -> p n d", n=H))
-
-        def mm2u(q, y):
-            codes, sc = ccodes[q]
-            up = psum.tile([P, 2, 256], F32, name=f"up{q}_{y}", tag="up", bufs=2)
-            for e in range(2):
-                n = 2 * y + e
-                nc.tensor.matmul_mx(out=up[:, e, :], lhsT=wqr_codes[:, n * P : (n + 1) * P].bitcast(FP8X4),
+        def mm2u(i):
+            codes, sc = cq[i]
+            up = psum.tile([P, H, P], F32, name=f"up{i}", tag="up")
+            for n in range(H):
+                nc.tensor.matmul_mx(out=up[:, n, :], lhsT=wqr_codes[:, n * P : (n + 1) * P].bitcast(FP8X4),
                                     lhsT_scale=wqr_sc[:, n * P : (n + 1) * P],
                                     rhs=codes[:].bitcast(FP8X4), rhs_scale=sc[:], start=True, stop=True)
-            ups[q, y] = up
+            ups[i] = up
 
-        usb = {}
+        def mm2a(i):
+            codes, sc = cq[i]
+            ap_ = psum.tile([P, 512], F32, name=f"ap{i}", tag="ra")
+            nc.tensor.matmul_mx(out=ap_[:], lhsT=codes[:].bitcast(FP8X4), lhsT_scale=sc[:],
+                                rhs=wq_codes[:].bitcast(FP8X4), rhs_scale=wq_sc[:], start=True, stop=True)
+            aps[i] = ap_
 
-        def u_copy(q, y):
-            us = work.tile([P, 2, 256], F32, name=f"us{q}_{y}", tag="us", align_bytes=64)
-            nc.scalar.copy(out=us[:], in_=ups[q, y][:])
-            usb[q, y] = us
+        def a_copy(i):
+            if i % 2 == 0:
+                o = work.tile([P, H, 2, 2 * DH], F32, name=f"o{i}", tag="o", bufs=4, align_bytes=64)
+                osb[i // 2] = o
+            nc.scalar.copy(out=osb[i // 2][:, :, i % 2, 0:DH], in_=aps[i][:].rearrange("p (n d) -> p n d", n=H))
 
-        def rope_mul(q, y):
-            t = work.tile([P, 2, 2, 256], F32, name=f"t{q}_{y}", tag="t", bufs=4, align_bytes=64)
-            k = q % 4
-            cs = tab[:, k // 2, :, 256 * (k % 2) : 256 * (k % 2 + 1)]
-            if (q, y) in usb:
-                nc.gpsimd.tensor_tensor(out=t[:, 1], in0=usb[q, y][:],
-                                        in1=cs[:, 1, :].unsqueeze(1).to_broadcast([P, 2, 256]), op=ALU.mult)
-                nc.vector.tensor_tensor(out=t[:, 0], in0=ups[q, y][:],
-                                        in1=cs[:, 0, :].unsqueeze(1).to_broadcast([P, 2, 256]), op=ALU.mult)
-            else:
-                nc.vector.tensor_tensor(out=t[:], in0=ups[q, y][:].unsqueeze(1).to_broadcast([P, 2, 2, 256]),
-                                        in1=cs.unsqueeze(2).to_broadcast([P, 2, 2, 256]), op=ALU.mult)
-            ts[q, y] = t
+        def rope_mul(i):
+            t = work.tile([P, 2, H, P], F32, name=f"t{i}", tag="t", align_bytes=64)
+            k = i % 8
+            cs = tab[:, k // 4, :, P * (k % 4) : P * (k % 4 + 1)]
+            nc.vector.tensor_tensor(out=t[:], in0=ups[i][:].unsqueeze(1).to_broadcast([P, 2, H, P]),
+                                    in1=cs.unsqueeze(2).to_broadcast([P, 2, H, P]), op=ALU.mult)
+            ts[i] = t
 
-        def r_transpose(q, y):
-            rp = psum.tile([P, 2, 2, P], F32, name=f"rp{q}_{y}", tag="ra", bufs=2)
-            for e in range(2):
-                for i in range(2):
-                    cols = slice(i * P, (i + 1) * P)
-                    nc.tensor.matmul(rp[:, e, i, :], lhsT=ts[q, y][:, 0, e, cols], rhs=ident[:], is_transpose=True,
-                                     start=True, stop=False)
-                    nc.tensor.matmul(rp[:, e, i, :], lhsT=ts[q, y][:, 1, e, cols], rhs=perm[:], is_transpose=True,
-                                     start=False, stop=True)
-            rps[q, y] = rp
+        def r_transpose(i):
+            rp = psum.tile([P, H, P], F32, name=f"rp{i}", tag="ra")
+            for n in range(H):
+                nc.tensor.matmul(rp[:, n, :], lhsT=ts[i][:, 0, n, :], rhs=ident[:], is_transpose=True,
+                                 start=True, stop=False)
+                nc.tensor.matmul(rp[:, n, :], lhsT=ts[i][:, 1, n, :], rhs=perm[:], is_transpose=True,
+                                 start=False, stop=True)
+            rps[i] = rp
 
-        def r_copy(q, y):
-            c, j = q // 2, 2 * (q % 2)
-            (V if (y == 1 and q in RV) else A)(out=osb[c][:, 2 * y : 2 * y + 2, j : j + 2, DH : 2 * DH], in_=rps[q, y][:])
+        def r_copy(i):
+            nc.scalar.copy(out=osb[i // 2][:, :, i % 2, DH : 2 * DH], in_=rps[i][:])
 
-        def store(q, y):
-            c = q // 2
-            j0, j1 = 2 * (q % 2), 2 * (q % 2) + 2
+        def store(i):
+            c = i // 4
             b, half = c // 2, c % 2
-            for n in (2 * y, 2 * y + 1):
+            if i < NT - 2:
+                if i % 2 == 0:
+                    return
+                j0, j1, k0, k1 = i % 4 - 1, i % 4 + 1, 0, 2
+            else:
+                j0, j1, k0, k1 = i % 4, i % 4 + 1, i % 2, i % 2 + 1
+            for n in range(H):
                 nc.sync.dma_start(
                     out=out[b, n, half * 512 : (half + 1) * 512, :].rearrange("(p j) d -> p j d", j=4)[:, j0:j1, :],
-                    in_=osb[c][:, n, j0:j1, :])
+                    in_=osb[i // 2][:, n, k0:k1, :])
 
-        def units(q):
-            return [(q, 0), (q, 1)] if 0 <= q < NP else []
+        def ok(i):
+            return 0 <= i < NT
 
-        def rope_end(q):
-            for un in units(q):
-                r_transpose(*un)
-            for un in units(q):
-                r_copy(*un)
-                store(*un)
+        def step(s):
+            if ok(s - 1):
+                h_quant(s - 1)
+            if ok(s - 4):
+                r_transpose(s - 4)
+                r_copy(s - 4)
+                store(s - 4)
+            if ok(s):
+                h_transpose(s)
+                h_copy(s)
+            if ok(s - 3):
+                rope_mul(s - 3)
+            if ok(s - 1):
+                mm1(s - 1)
+                c_copy(s - 1)
+            if ok(s - 2):
+                c_quant(s - 2)
+            widen_to(WT(s))
+            if ok(s - 2):
+                mm2u(s - 2)
+                mm2a(s - 2)
+                a_copy(s - 2)
 
-        def step(q):
-            if q < NP:
-                h_transpose(q)
-                h_copy(q)
-            if 0 <= q - 1 < NP:
-                mm1(q - 1)
-            for un in units(q - 2):
-                if un in OFF:
-                    u_copy(*un)
-            for un in units(q - 2):
-                rope_mul(*un)
-            if 0 <= q - 1 < NP:
-                c_copy(q - 1)
-            for un in units(q - 3):
-                r_transpose(*un)
-            for un in units(q - 3):
-                r_copy(*un)
-                store(*un)
-            widen_to(WT(q) - WB)
-            if 0 <= q - 1 < NP:
-                c_quant(q - 1)
-            widen_to(WT(q))
-            if q < NP:
-                h_quant(q)
-            for un in units(q - 1):
-                mm2u(*un)
-            if q == NP and RE:
-                rope_end(q - 2)
-            if 0 <= q - 1 < NP:
-                mm2a(q - 1)
-                a_copy(q - 1)
 
-        if PS < 0:
-            tables_s()
+        turns_v(0)
+        whole_v(0)
+        widen_to(1)
+        frac_v(0)
+        tables_s(0)
         widen_to(2)
+        h_transpose(0)
+        h_copy(0)
+        h_transpose(1)
+        h_copy(1)
         wcq_copy(V, 0)
         wcq_copy(V, 1)
         wcq_quant(0)
         wcq_quant(1)
-        widen_to(W0)
-        for q in range(0, NP + 1):
-            if q == PQ:
-                w_copy(A, wq_g, wq_raw)
-            if q == PR:
-                w_copy(A, wqr_g, wqr_raw)
-            if q == PS:
-                tables_s()
-            if q == 1:
-                nc.vector.quantize_mx(out=wq_codes[:].bitcast(FP8X4), scales=wq_sc[:], in_=wq_g[:])
-                nc.vector.quantize_mx(out=wqr_codes[:].bitcast(FP8X4), scales=wqr_sc[:], in_=wqr_g[:])
-            step(q)
-        if not RE:
-            rope_end(NP - 2)
-        for un in units(NP - 1):
-            rope_mul(*un)
-        rope_end(NP - 1)
+        h_quant(0)
+        w_copy(A, wqr_g, wqr_raw)
+        mm1(0)
+        widen_to(3)
+        h_quant(1)
+        c_copy(0)
+        nc.vector.quantize_mx(out=wqr_codes[:].bitcast(FP8X4), scales=wqr_sc[:], in_=wqr_g[:])
+        w_copy(A, wq_g, wq_raw)
+        c_quant(0)
+        turns_v(1)
+        whole_v(1)
+        h_transpose(2)
+        h_copy(2)
+        mm1(1)
+        c_copy(1)
+        widen_to(4)
+        frac_v(1)
+        nc.vector.quantize_mx(out=wq_codes[:].bitcast(FP8X4), scales=wq_sc[:], in_=wq_g[:])
+        mm2u(0)
+        mm2a(0)
+        a_copy(0)
+        tables_s(1)
+        for s in range(3, NT + 4):
+            step(s)

@@ -103,8 +103,6 @@ def tile_mla_pa_t_kernel(tc, h_bytes, h_scale, w_cq, w_q, w_qr, out):
         nc.scalar.copy(out=scv[:, 1], in_=sc_ps[1][:].rearrange("p c q -> p q c"))
         thc = keep.tile([P, 1], F32, name="thc")
         nc.vector.tensor_copy(out=thc[:], in_=th_ps[:, 0:1])
-        nc.vector.tensor_copy(out=scv[:, 0], in_=sc_ps[0][:].rearrange("p c q -> p q c"))
-
         turns = keep.tile([P, S], F32, name="turns", align_bytes=64)
         whole = keep.tile([P, S], I32, name="whole", align_bytes=64)
         frac = keep.tile([P, S], F32, name="frac", align_bytes=64)
@@ -129,6 +127,10 @@ def tile_mla_pa_t_kernel(tc, h_bytes, h_scale, w_cq, w_q, w_qr, out):
             nc.scalar.activation(out=fabs[:, cols], in_=frac[:, cols], func=ACT.Abs)
             nc.scalar.activation(out=tab[:, h, 0, :], in_=fabs[:, cols], func=ACT.Sin, scale=-2.0 * math.pi,
                                  bias=hpi2[:, 0:1])
+        turns_v(0)
+        turns_v(1)
+        nc.vector.tensor_copy(out=scv[:, 0], in_=sc_ps[0][:].rearrange("p c q -> p q c"))
+
 
         wcq_codes = keep.tile([P, 2, CQ], U32, name="wcq_codes", align_bytes=64)
         wcq_sc = keep.tile([P, 2, CQ], U8, name="wcq_sc", align_bytes=64)
@@ -150,7 +152,7 @@ def tile_mla_pa_t_kernel(tc, h_bytes, h_scale, w_cq, w_q, w_qr, out):
         def w_copy(copy, grouped, raw):
             copy(out=grouped[:].rearrange("p (n j) -> p n j", j=4), in_=raw[:].rearrange("p j n -> p n j"))
 
-        xb, hps, grp, hq, cps, cgs, cq, ups, ts, rps, aps, osb = ({} for k in range(12))
+        xb, hps, grp, hq, cps, cgs, cq, ups, ts, rps, aps, osb, u3s = ({} for k in range(13))
 
         def widen_to(n):
             while len(xb) < min(n, NT):
@@ -230,9 +232,21 @@ def tile_mla_pa_t_kernel(tc, h_bytes, h_scale, w_cq, w_q, w_qr, out):
             t = work.tile([P, 2, H, P], F32, name=f"t{i}", tag="t", align_bytes=64)
             k = i % 8
             cs = tab[:, k // 4, :, P * (k % 4) : P * (k % 4 + 1)]
-            nc.vector.tensor_tensor(out=t[:], in0=ups[i][:].unsqueeze(1).to_broadcast([P, 2, H, P]),
-                                    in1=cs.unsqueeze(2).to_broadcast([P, 2, H, P]), op=ALU.mult)
+            G = H - 1
+            nc.vector.tensor_tensor(out=t[:, :, 0:G, :], in0=ups[i][:, 0:G, :].unsqueeze(1).to_broadcast([P, 2, G, P]),
+                                    in1=cs.unsqueeze(2).to_broadcast([P, 2, G, P]), op=ALU.mult)
+            nc.gpsimd.tensor_tensor(out=t[:, :, G, :], in0=u3s[i][:].unsqueeze(1).to_broadcast([P, 2, P]), in1=cs,
+                                    op=ALU.mult)
             ts[i] = t
+
+        def tick(i):
+            word = work.tile([P, 1], U32, name=f"tick{i}", tag="tick")
+            nc.gpsimd.tensor_copy(out=word[:], in_=cq[i][0][:, 0:1])
+
+        def u3_copy(i):
+            u3 = work.tile([P, P], F32, name=f"u3_{i}", tag="u3", align_bytes=64)
+            nc.scalar.copy(out=u3[:], in_=ups[i][:, H - 1, :])
+            u3s[i] = u3
 
         def r_transpose(i):
             rp = psum.tile([P, H, P], F32, name=f"rp{i}", tag="ra")
@@ -249,7 +263,7 @@ def tile_mla_pa_t_kernel(tc, h_bytes, h_scale, w_cq, w_q, w_qr, out):
         def store(i):
             c = i // 4
             b, half = c // 2, c % 2
-            if i < NT - 2:
+            if i < NT - 4:
                 if i % 2 == 0:
                     return
                 j0, j1, k0, k1 = i % 4 - 1, i % 4 + 1, 0, 2
@@ -266,38 +280,39 @@ def tile_mla_pa_t_kernel(tc, h_bytes, h_scale, w_cq, w_q, w_qr, out):
         def step(s):
             if ok(s - 1):
                 h_quant(s - 1)
+            if ok(s - 2):
+                c_quant(s - 2)
+                tick(s - 2)
+            widen_to(WT(s))
+            if ok(s):
+                h_transpose(s)
+                h_copy(s)
             if ok(s - 4):
                 r_transpose(s - 4)
                 r_copy(s - 4)
                 store(s - 4)
-            if ok(s):
-                h_transpose(s)
-                h_copy(s)
             if ok(s - 3):
                 rope_mul(s - 3)
             if ok(s - 1):
                 mm1(s - 1)
                 c_copy(s - 1)
-            if ok(s - 2):
-                c_quant(s - 2)
-            widen_to(WT(s))
+
             if ok(s - 2):
                 mm2u(s - 2)
                 mm2a(s - 2)
+                u3_copy(s - 2)
                 a_copy(s - 2)
 
-
-        turns_v(0)
         whole_v(0)
         widen_to(1)
         frac_v(0)
+        wcq_copy(A, 0)
         tables_s(0)
         widen_to(2)
         h_transpose(0)
         h_copy(0)
         h_transpose(1)
         h_copy(1)
-        wcq_copy(V, 0)
         wcq_copy(V, 1)
         wcq_quant(0)
         wcq_quant(1)
@@ -310,7 +325,6 @@ def tile_mla_pa_t_kernel(tc, h_bytes, h_scale, w_cq, w_q, w_qr, out):
         nc.vector.quantize_mx(out=wqr_codes[:].bitcast(FP8X4), scales=wqr_sc[:], in_=wqr_g[:])
         w_copy(A, wq_g, wq_raw)
         c_quant(0)
-        turns_v(1)
         whole_v(1)
         h_transpose(2)
         h_copy(2)
@@ -321,6 +335,7 @@ def tile_mla_pa_t_kernel(tc, h_bytes, h_scale, w_cq, w_q, w_qr, out):
         nc.vector.quantize_mx(out=wq_codes[:].bitcast(FP8X4), scales=wq_sc[:], in_=wq_g[:])
         mm2u(0)
         mm2a(0)
+        u3_copy(0)
         a_copy(0)
         tables_s(1)
         for s in range(3, NT + 4):

from contextlib import ExitStack
import math

import concourse.mybir as mybir
from concourse.masks import make_identity

F32 = mybir.dt.float32
BF16 = mybir.dt.bfloat16
U32 = mybir.dt.uint32
I32 = mybir.dt.int32
U8 = mybir.dt.uint8
E4M3 = mybir.dt.float8_e4m3fn
FP8X4 = mybir.dt.float8_e4m3fn_x4
ALU = mybir.AluOpType
ACT = mybir.ActivationFunctionType

B, S, D, H, DH, CQ = 4, 1024, 1024, 4, 128, 512
P = 128
NT = B * S // P
NC = NT // 4


def WT(s):
    return s + 3


FLOPS = 2 * B * S * (D * CQ + 2 * CQ * H * DH) + 3 * B * S * H * DH


def tile_mla_pa_t_kernel(tc, h_bytes, h_scale, w_cq, w_q, w_qr, out):
    nc = tc.nc
    V = nc.vector.tensor_copy
    A = nc.scalar.copy
    with ExitStack() as ctx:
        keep = ctx.enter_context(tc.tile_pool(name="keep", bufs=1))
        work = ctx.enter_context(tc.tile_pool(name="work", bufs=3))
        psum = ctx.enter_context(tc.psum_pool(name="psum", bufs=2))
        ctx.enter_context(tc.manual_schedule())

        hb = [keep.tile([P, 4, D], U8, name=f"hb{c}", align_bytes=64) for c in range(NC)]

        def load_h(c, j0, j1):
            b, half = c // 2, c % 2
            nc.sync.dma_start(
                out=hb[c][:, j0:j1, :],
                in_=h_bytes[b, half * 512 : (half + 1) * 512, :].rearrange("(p j) k -> p j k", j=4)[:, j0:j1, :])

        sv = keep.tile([P, 8], F32, name="sv")
        nc.sync.dma_start(out=sv[:], in_=h_scale.rearrange("a b (p c) -> p (a b c)", c=8))
        wcq_raw = [keep.tile([P, 4, CQ], BF16, name=f"wcq_raw{g}", align_bytes=64) for g in range(2)]
        wq_raw = keep.tile([P, 4, H * DH], BF16, name="wq_raw", align_bytes=64)
        wqr_raw = keep.tile([P, 4, H * DH], BF16, name="wqr_raw", align_bytes=64)

        def load_wcq(g):
            nc.sync.dma_start(out=wcq_raw[g][:],
                              in_=w_cq[g * 512 : (g + 1) * 512, :].rearrange("(p j) c -> p j c", j=4))

        load_h(0, 0, 2)
        load_wcq(0)
        load_wcq(1)
        load_h(0, 2, 4)
        nc.sync.dma_start(out=wqr_raw[:], in_=w_qr.rearrange("(p j) c -> p j c", j=4))
        nc.sync.dma_start(out=wq_raw[:], in_=w_q.rearrange("(p j) c -> p j c", j=4))
        for c in range(1, NC):
            load_h(c, 0, 4)

        ident = keep.tile([P, P], F32, name="ident", align_bytes=64)
        make_identity(nc, ident[:])
        warm = keep.tile([P, 1], F32, name="warm")
        nc.gpsimd.memset(warm[:], 0.0)
        warm2 = keep.tile([P, 1], F32, name="warm2")
        nc.scalar.activation(out=warm2[:], in_=warm[:], func=ACT.Sin)
        s_row = keep.tile([P, S], F32, name="s_row", align_bytes=64)
        nc.gpsimd.iota(s_row[:].rearrange("p (c j q) -> p c j q", c=2, j=4), pattern=[[512, 2], [1, 4], [4, 128]],
                       base=0, channel_multiplier=0, allow_small_or_imprecise_dtypes=True)
        th = keep.tile([P, 64], F32, name="th")
        nc.vector.memset(th[:, 0:1], 1.0)
        w = 1
        while w < 64:
            nc.vector.tensor_scalar(out=th[:, w : 2 * w], in0=th[:, 0:w], scalar1=10000.0 ** (-w / 64.0),
                                    scalar2=None, op0=ALU.mult)
            w *= 2
        th2 = keep.tile([P, P], F32, name="th2", align_bytes=64)
        for e in range(2):
            nc.vector.tensor_scalar(out=th2[:].rearrange("p (i two) -> p two i", two=2)[:, e, :], in0=th[:],
                                    scalar1=(1.0 - 2.0 * e) / (2.0 * math.pi), scalar2=None, op0=ALU.mult)
        hpi = keep.tile([P, 1], F32, name="hpi")
        nc.gpsimd.memset(hpi[:], 1.0)
        hpi2 = keep.tile([P, 1], F32, name="hpi2")
        nc.gpsimd.tensor_scalar(out=hpi2[:], in0=hpi[:], scalar1=math.pi / 2, scalar2=None, op0=ALU.mult)
        perm = keep.tile([P, P], F32, name="perm", align_bytes=64)
        for e in range(2):
            nc.gpsimd.tensor_copy(out=perm[:].rearrange("p (i two) -> p two i", two=2)[:, e, :],
                                  in_=ident[:].rearrange("p (i two) -> p two i", two=2)[:, 1 - e, :])
        th_ps = psum.tile([P, P], F32, name="th_ps", tag="ra")
        nc.tensor.transpose(th_ps[:], th2[:], ident[:])

        scale = keep.tile([P, D], F32, name="scale", align_bytes=64)
        sc_ps = [psum.tile([P, 4, P], F32, name=f"sc_ps{k}", tag="ht") for k in range(2)]
        for k in range(8):
            nc.tensor.transpose(sc_ps[k // 4][:, k % 4, :], sv[:, k : k + 1].to_broadcast([P, P]), ident[:])
        scv = scale[:].rearrange("p (q k c) -> p k q c", k=2, c=4)
        nc.scalar.copy(out=scv[:, 1], in_=sc_ps[1][:].rearrange("p c q -> p q c"))
        thc = keep.tile([P, 1], F32, name="thc")
        nc.vector.tensor_copy(out=thc[:], in_=th_ps[:, 0:1])
        turns = keep.tile([P, S], F32, name="turns", align_bytes=64)
        whole = keep.tile([P, S], I32, name="whole", align_bytes=64)
        frac = keep.tile([P, S], F32, name="frac", align_bytes=64)
        fabs = keep.tile([P, S], F32, name="fabs", align_bytes=64)
        tab = keep.tile([P, 2, 2, 512], F32, name="tab", align_bytes=64)

        def turns_v(h):
            cols = slice(512 * h, 512 * (h + 1))
            nc.vector.tensor_scalar(out=turns[:, cols], in0=s_row[:, cols], scalar1=thc[:, 0:1], scalar2=None,
                                    op0=ALU.mult)
        def whole_v(h):
            cols = slice(512 * h, 512 * (h + 1))
            nc.vector.tensor_copy(out=whole[:, cols], in_=turns[:, cols])

        def frac_v(h):
            cols = slice(512 * h, 512 * (h + 1))
            nc.vector.tensor_tensor(out=frac[:, cols], in0=turns[:, cols], in1=whole[:, cols], op=ALU.subtract)

        def tables_s(h):
            cols = slice(512 * h, 512 * (h + 1))
            nc.scalar.activation(out=tab[:, h, 1, :], in_=frac[:, cols], func=ACT.Sin, scale=2.0 * math.pi)
            nc.scalar.activation(out=fabs[:, cols], in_=frac[:, cols], func=ACT.Abs)
            nc.scalar.activation(out=tab[:, h, 0, :], in_=fabs[:, cols], func=ACT.Sin, scale=-2.0 * math.pi,
                                 bias=hpi2[:, 0:1])
        turns_v(0)
        turns_v(1)
        nc.vector.tensor_copy(out=scv[:, 0], in_=sc_ps[0][:].rearrange("p c q -> p q c"))


        wcq_codes = keep.tile([P, 2, CQ], U32, name="wcq_codes", align_bytes=64)
        wcq_sc = keep.tile([P, 2, CQ], U8, name="wcq_sc", align_bytes=64)
        wq_codes = keep.tile([P, 512], U32, name="wq_codes", align_bytes=64)
        wq_sc = keep.tile([P, 512], U8, name="wq_sc", align_bytes=64)
        wqr_codes = keep.tile([P, 512], U32, name="wqr_codes", align_bytes=64)
        wqr_sc = keep.tile([P, 512], U8, name="wqr_sc", align_bytes=64)
        wcq_g = [keep.tile([P, 4 * CQ], BF16, name=f"wcq_g{g}", align_bytes=64) for g in range(2)]
        wq_g = keep.tile([P, 2048], BF16, name="wq_g", align_bytes=64)
        wqr_g = keep.tile([P, 2048], BF16, name="wqr_g", align_bytes=64)

        def wcq_copy(copy, g):
            copy(out=wcq_g[g][:].rearrange("p (t m j) -> p t m j", t=4, j=4),
                 in_=wcq_raw[g][:].rearrange("p j (m t) -> p t m j", t=4))

        def wcq_quant(g):
            nc.vector.quantize_mx(out=wcq_codes[:, g, :].bitcast(FP8X4), scales=wcq_sc[:, g, :], in_=wcq_g[g][:])

        def w_copy(copy, grouped, raw):
            copy(out=grouped[:].rearrange("p (n j) -> p n j", j=4), in_=raw[:].rearrange("p j n -> p n j"))

        xb, hps, grp, hq, cps, cgs, cq, ups, ts, rps, aps, osb, u3s = ({} for k in range(13))

        def widen_to(n):
            while len(xb) < min(n, NT):
                i = len(xb)
                x = work.tile([P, D], BF16, name=f"x{i}", tag="x", bufs=8, align_bytes=64)
                nc.vector.tensor_tensor(out=x[:], in0=hb[i // 4][:, i % 4, :].bitcast(E4M3), in1=scale[:], op=ALU.mult)
                xb[i] = x

        def h_transpose(i):
            ht = psum.tile([P, 2, 2, P], F32, name=f"ht{i}", tag="ht")
            words = xb[i][:].bitcast(F32)
            for g in range(2):
                for u in range(2):
                    nc.tensor.transpose(ht[:, g, u, :], words[:, 256 * g + u : 256 * (g + 1) : 2], ident[:])
            hps[i] = ht

        def h_copy(i):
            gt = work.tile([P, D], BF16, name=f"g{i}", tag="g", align_bytes=64)
            nc.scalar.copy(out=gt[:].bitcast(F32).rearrange("p (g n u) -> p g n u", g=2, u=2),
                           in_=hps[i][:].rearrange("p g u n -> p g n u"))
            grp[i] = gt

        def h_quant(i):
            codes = work.tile([P, 256], U32, name=f"hc{i}", tag="hc", align_bytes=64)
            sc = work.tile([P, 256], U8, name=f"hs{i}", tag="hs", align_bytes=64)
            nc.vector.quantize_mx(out=codes[:].bitcast(FP8X4), scales=sc[:], in_=grp[i][:])
            hq[i] = (codes, sc)

        def mm1(i):
            codes, sc = hq[i]
            cp = psum.tile([P, 4, P], F32, name=f"cp{i}", tag="cp")
            for t in range(4):
                for g in range(2):
                    cols = slice(g * P, (g + 1) * P)
                    nc.tensor.matmul_mx(
                        out=cp[:, t, :],
                        lhsT=wcq_codes[:, g, t * P : (t + 1) * P].bitcast(FP8X4),
                        lhsT_scale=wcq_sc[:, g, t * P : (t + 1) * P],
                        rhs=codes[:, cols].bitcast(FP8X4), rhs_scale=sc[:, cols],
                        start=(g == 0), stop=(g == 1))
            cps[i] = cp

        def c_copy(i):
            cg = work.tile([P, 512], BF16, name=f"cg{i}", tag="cg", align_bytes=64)
            nc.scalar.copy(out=cg[:].rearrange("p (n t) -> p n t", t=4), in_=cps[i][:].rearrange("p t n -> p n t"))
            cgs[i] = cg

        def c_quant(i):
            codes = work.tile([P, P], U32, name=f"cc{i}", tag="cc", align_bytes=64)
            sc = work.tile([P, P], U8, name=f"cs{i}", tag="cs", align_bytes=64)
            nc.vector.quantize_mx(out=codes[:].bitcast(FP8X4), scales=sc[:], in_=cgs[i][:])
            cq[i] = (codes, sc)

        def mm2u(i):
            codes, sc = cq[i]
            up = psum.tile([P, H, P], F32, name=f"up{i}", tag="up")
            for n in range(H):
                nc.tensor.matmul_mx(out=up[:, n, :], lhsT=wqr_codes[:, n * P : (n + 1) * P].bitcast(FP8X4),
                                    lhsT_scale=wqr_sc[:, n * P : (n + 1) * P],
                                    rhs=codes[:].bitcast(FP8X4), rhs_scale=sc[:], start=True, stop=True)
            ups[i] = up

        def mm2a(i):
            codes, sc = cq[i]
            ap_ = psum.tile([P, 512], F32, name=f"ap{i}", tag="ra")
            nc.tensor.matmul_mx(out=ap_[:], lhsT=codes[:].bitcast(FP8X4), lhsT_scale=sc[:],
                                rhs=wq_codes[:].bitcast(FP8X4), rhs_scale=wq_sc[:], start=True, stop=True)
            aps[i] = ap_

        def a_copy(i):
            if i % 2 == 0:
                o = work.tile([P, H, 2, 2 * DH], F32, name=f"o{i}", tag="o", bufs=4, align_bytes=64)
                osb[i // 2] = o
            nc.scalar.copy(out=osb[i // 2][:, :, i % 2, 0:DH], in_=aps[i][:].rearrange("p (n d) -> p n d", n=H))

        def rope_mul(i):
            t = work.tile([P, 2, H, P], F32, name=f"t{i}", tag="t", align_bytes=64)
            k = i % 8
            cs = tab[:, k // 4, :, P * (k % 4) : P * (k % 4 + 1)]
            G = H - 1
            nc.vector.tensor_tensor(out=t[:, :, 0:G, :], in0=ups[i][:, 0:G, :].unsqueeze(1).to_broadcast([P, 2, G, P]),
                                    in1=cs.unsqueeze(2).to_broadcast([P, 2, G, P]), op=ALU.mult)
            nc.gpsimd.tensor_tensor(out=t[:, :, G, :], in0=u3s[i][:].unsqueeze(1).to_broadcast([P, 2, P]), in1=cs,
                                    op=ALU.mult)
            ts[i] = t

        def tick(i):
            word = work.tile([P, 1], U32, name=f"tick{i}", tag="tick")
            nc.gpsimd.tensor_copy(out=word[:], in_=cq[i][0][:, 0:1])

        def u3_copy(i):
            u3 = work.tile([P, P], F32, name=f"u3_{i}", tag="u3", align_bytes=64)
            nc.scalar.copy(out=u3[:], in_=ups[i][:, H - 1, :])
            u3s[i] = u3

        def r_transpose(i):
            rp = psum.tile([P, H, P], F32, name=f"rp{i}", tag="ra")
            for n in range(H):
                nc.tensor.matmul(rp[:, n, :], lhsT=ts[i][:, 0, n, :], rhs=ident[:], is_transpose=True,
                                 start=True, stop=False)
                nc.tensor.matmul(rp[:, n, :], lhsT=ts[i][:, 1, n, :], rhs=perm[:], is_transpose=True,
                                 start=False, stop=True)
            rps[i] = rp

        def r_copy(i):
            nc.scalar.copy(out=osb[i // 2][:, :, i % 2, DH : 2 * DH], in_=rps[i][:])

        def store(i):
            c = i // 4
            b, half = c // 2, c % 2
            if i < NT - 4:
                if i % 2 == 0:
                    return
                j0, j1, k0, k1 = i % 4 - 1, i % 4 + 1, 0, 2
            else:
                j0, j1, k0, k1 = i % 4, i % 4 + 1, i % 2, i % 2 + 1
            for n in range(H):
                nc.sync.dma_start(
                    out=out[b, n, half * 512 : (half + 1) * 512, :].rearrange("(p j) d -> p j d", j=4)[:, j0:j1, :],
                    in_=osb[i // 2][:, n, k0:k1, :])

        def ok(i):
            return 0 <= i < NT

        def step(s):
            if ok(s - 1):
                h_quant(s - 1)
            if ok(s - 2):
                c_quant(s - 2)
                tick(s - 2)
            widen_to(WT(s))
            if ok(s):
                h_transpose(s)
                h_copy(s)
            if ok(s - 4):
                r_transpose(s - 4)
                r_copy(s - 4)
                store(s - 4)
            if ok(s - 3):
                rope_mul(s - 3)
            if ok(s - 1):
                mm1(s - 1)
                c_copy(s - 1)

            if ok(s - 2):
                mm2u(s - 2)
                mm2a(s - 2)
                u3_copy(s - 2)
                a_copy(s - 2)

        whole_v(0)
        widen_to(1)
        frac_v(0)
        wcq_copy(A, 0)
        tables_s(0)
        widen_to(2)
        h_transpose(0)
        h_copy(0)
        h_transpose(1)
        h_copy(1)
        wcq_copy(V, 1)
        wcq_quant(0)
        wcq_quant(1)
        h_quant(0)
        w_copy(A, wqr_g, wqr_raw)
        mm1(0)
        widen_to(3)
        h_quant(1)
        c_copy(0)
        nc.vector.quantize_mx(out=wqr_codes[:].bitcast(FP8X4), scales=wqr_sc[:], in_=wqr_g[:])
        w_copy(A, wq_g, wq_raw)
        c_quant(0)
        whole_v(1)
        h_transpose(2)
        h_copy(2)
        mm1(1)
        c_copy(1)
        widen_to(4)
        frac_v(1)
        nc.vector.quantize_mx(out=wq_codes[:].bitcast(FP8X4), scales=wq_sc[:], in_=wq_g[:])
        mm2u(0)
        mm2a(0)
        u3_copy(0)
        a_copy(0)
        tables_s(1)
        for s in range(3, NT + 4):
            step(s)
